import numpy as np
import ml_dtypes


def mxq(x, axis, fmt="e4m3"):
    dtype, down = {"e4m3": (ml_dtypes.float8_e4m3fn, 7), "e5m2": (ml_dtypes.float8_e5m2, 14)}[fmt]
    v = np.moveaxis(np.asarray(x, np.float32).astype(ml_dtypes.bfloat16).astype(np.float64), axis, -1)
    blocks = v.reshape(v.shape[:-1] + (-1, 32))
    amax = np.abs(blocks).max(-1, keepdims=True)
    byte = np.maximum(np.where(amax > 0, np.frexp(amax)[1] - 1 + 127, 0) - down, 1)
    scale = np.exp2(byte - 127.0)
    codes = (blocks / scale).astype(np.float32).astype(dtype).astype(np.float64)
    return np.moveaxis((codes * scale).reshape(v.shape), -1, axis)


WIDE = False


def mx_kscale(k):
    if not WIDE:
        return np.ones(k)
    levels = np.array([10, -10, 5, -5, 0])
    a = np.random.permutation(np.resize(levels, k // 512 * 4)).reshape(k // 512, 4)
    idx = np.arange(k)
    return np.exp2(a[idx // 512, idx % 128 // 32])


BF16 = ml_dtypes.bfloat16


def bf(x):
    return np.asarray(x, np.float32).astype(BF16)


def f64(x):
    return np.asarray(x).astype(np.float64)


B, N, K, D, L = 1, 1024, 16, 512, 512


def setup_inputs():
    s = mx_kscale(D)
    limit = np.sqrt(6.0 / (D + L))
    lone = np.random.random((B, N, 1)) < 0.125
    a = (0.3 + 0.7 * np.random.random((B, N, K + 1))) * np.where(lone, 0.4 / (K + 1), 1.0)
    return {"targets": bf(np.random.standard_normal((B, N, D)) * s),
            "neighbors": bf(np.random.standard_normal((B, N, K, D)) * s),
            "a": bf(a),
            "kernel": bf(np.random.uniform(-limit, limit, (D, L)) / s[:, None])}


def reference(targets, neighbors, a, kernel):
    neighborhood = np.concatenate([f64(targets)[..., None, :], f64(neighbors)], axis=-2)
    y = (mxq(neighborhood, 3, "e4m3") @ mxq(f64(kernel), 0, "e4m3")).sum(axis=-2)
    factor = f64(a).sum(axis=-1, keepdims=True)
    factor = np.where(factor > 0.5, factor, np.ones_like(factor))
    y = y / factor
    return np.maximum(y, 0.0)

@@ -1,0 +1,164 @@
+from contextlib import ExitStack
+
+import concourse.mybir as mybir
+from concourse.masks import make_identity
+
+F32 = mybir.dt.float32
+BF16 = mybir.dt.bfloat16
+U32 = mybir.dt.uint32
+U8 = mybir.dt.uint8
+FP8X4 = mybir.dt.float8_e4m3fn_x4
+ALU = mybir.AluOpType
+ACT = mybir.ActivationFunctionType
+
+P = 128
+NODES = 1024
+NEIGH = 16
+MEMBERS = NEIGH + 1
+D = 512
+L = 512
+TILES = NODES // P
+UNITS = TILES * MEMBERS
+BANKS = UNITS // 2
+ROUND_BANKS = [2, 2] + [4] * 16
+VECTOR_EVAC = (1,)
+
+FLOPS = 2 * NODES * MEMBERS * D * L
+
+assert sum(ROUND_BANKS) == BANKS
+
+
+def tile_singlegcnlayer_kernel(tc, targets, neighbors, a, kernel, out):
+    nc = tc.nc
+    tgt_v = targets.flatten_outer_dims().rearrange("(p t) k -> p (t k)", p=P)
+    nb_v = neighbors.flatten_outer_dims().rearrange("(p r) k -> p (r k)", p=P)
+    a_v = a.flatten_outer_dims().rearrange("(p t) m -> p (t m)", p=P)
+    w_v = kernel.rearrange("(u q e) c -> q u (e c)", u=2, e=2)
+    out_v = out.flatten_outer_dims().rearrange("(p t) l -> p t l", p=P)
+
+    rounds = []
+    first = 0
+    for n in ROUND_BANKS:
+        rounds.append(list(range(first, first + n)))
+        first += n
+
+    with ExitStack() as ctx:
+        keep = ctx.enter_context(tc.tile_pool(name="keep", bufs=1))
+        gpool = ctx.enter_context(tc.tile_pool(name="gpool", bufs=8))
+        cpool = ctx.enter_context(tc.tile_pool(name="cpool", bufs=12))
+        psum_t = ctx.enter_context(tc.psum_pool(name="psum_t", bufs=6))
+        psum_a = ctx.enter_context(tc.psum_pool(name="psum_a", bufs=2))
+        ctx.enter_context(tc.manual_schedule())
+
+        ident = keep.tile([P, P], F32, name="ident")
+        make_identity(nc, ident[:])
+
+        w_raw = keep.tile([P, 4, L], BF16, name="w_raw")
+        nc.sync.dma_start(out=w_raw[:].rearrange("p (u e) c -> p u (e c)", e=2), in_=w_v)
+        tgt0 = keep.tile([P, D], BF16, name="tgt0")
+        nc.sync.dma_start(out=tgt0[:], in_=tgt_v[:, 0:D])
+        tgt_rest = keep.tile([P, (TILES - 1) * D], BF16, name="tgt_rest")
+        a_sb = keep.tile([P, TILES * MEMBERS], BF16, name="a_sb")
+
+        words = {}
+        words[0] = tgt0[:].bitcast(F32)
+        for t in range(1, TILES):
+            words[MEMBERS * t] = tgt_rest[:].bitcast(F32)[:, (t - 1) * 256 : t * 256]
+        for r, banks in enumerate(rounds):
+            units = [g for g in range(2 * banks[0], 2 * banks[-1] + 2) if g % MEMBERS != 0]
+            flat = [(g // MEMBERS) * NEIGH + g % MEMBERS - 1 for g in units]
+            chunk = keep.tile([P, len(units) * D], BF16, name="nb%d" % r)
+            if r == 3:
+                nc.sync.dma_start(out=tgt_rest[:], in_=tgt_v[:, D:])
+                nc.sync.dma_start(out=a_sb[:], in_=a_v)
+            nc.sync.dma_start(out=chunk[:], in_=nb_v[:, flat[0] * D : (flat[-1] + 1) * D])
+            for i, g in enumerate(units):
+                words[g] = chunk[:].bitcast(F32)[:, i * 256 : (i + 1) * 256]
+
+        w_grp = keep.tile([P, L, 4], BF16, name="w_grp", align_bytes=64)
+        nc.vector.tensor_copy(out=w_grp[:], in_=w_raw[:].rearrange("p t c -> p c t"))
+        w_codes = keep.tile([P, L], U32, name="w_codes", align_bytes=64)
+        w_scales = keep.tile([P, L], U8, name="w_scales", align_bytes=64)
+        nc.vector.quantize_mx(
+            out=w_codes[:].bitcast(FP8X4), scales=w_scales[:], in_=w_grp[:].rearrange("p c t -> p (c t)")
+        )
+
+        rinv = keep.tile([P, TILES], F32, name="rinv")
+
+        def degree():
+            deg = keep.tile([P, TILES], F32, name="deg")
+            nc.vector.tensor_reduce(
+                out=deg[:], in_=a_sb[:].rearrange("p (t m) -> p t m", m=MEMBERS), axis=mybir.AxisListType.X, op=ALU.add
+            )
+            big = keep.tile([P, TILES], F32, name="big")
+            nc.vector.tensor_scalar(out=big[:], in0=deg[:], scalar1=0.5, scalar2=None, op0=ALU.is_gt)
+            kept = keep.tile([P, TILES], F32, name="kept")
+            nc.vector.tensor_tensor(out=kept[:], in0=deg[:], in1=big[:], op=ALU.mult)
+            small = keep.tile([P, TILES], F32, name="small")
+            nc.vector.tensor_scalar(out=small[:], in0=big[:], scalar1=-1.0, scalar2=1.0, op0=ALU.mult, op1=ALU.add)
+            fac = keep.tile([P, TILES], F32, name="fac")
+            nc.vector.tensor_tensor(out=fac[:], in0=kept[:], in1=small[:], op=ALU.max)
+            nc.vector.reciprocal(out=rinv[:], in_=fac[:])
+
+        banks_xt = {}
+        banks_q = {}
+        accs = {}
+
+        def transposes(r):
+            for b in rounds[r]:
+                xt = psum_t.tile([P, 2, 2, P], F32, name="xt")
+                for j in range(2):
+                    for u in range(2):
+                        nc.tensor.transpose(xt[:, j, u, :], words[2 * b + j][:, u * P : (u + 1) * P], ident[:])
+                banks_xt[b] = xt
+
+        def quantise(r):
+            grouped = {}
+            for i, b in enumerate(rounds[r]):
+                grp = gpool.tile([P, 2 * D], BF16, name="grp", align_bytes=64)
+                dst = grp[:].bitcast(F32).rearrange("p (j n u) -> p j n u", j=2, u=2)
+                src = banks_xt[b][:].rearrange("p j u n -> p j n u")
+                if i in VECTOR_EVAC:
+                    nc.vector.tensor_copy(out=dst, in_=src)
+                else:
+                    nc.scalar.copy(out=dst, in_=src)
+                grouped[b] = grp
+            for b in rounds[r]:
+                codes = cpool.tile([P, 2 * P], U32, name="codes", align_bytes=64)
+                scales = cpool.tile([P, 2 * P], U8, name="scales", align_bytes=64)
+                nc.vector.quantize_mx(out=codes[:].bitcast(FP8X4), scales=scales[:], in_=grouped[b][:])
+                banks_q[b] = (codes, scales)
+
+        def products(r):
+            for b in rounds[r]:
+                codes, scales = banks_q[b]
+                for j in range(2):
+                    g = 2 * b + j
+                    t = g // MEMBERS
+                    m = g % MEMBERS
+                    if m == 0:
+                        acc = psum_a.tile([P, L], F32, name="acc")
+                        accs[t] = acc
+                    nc.tensor.matmul_mx(
+                        out=accs[t][:],
+                        lhsT=codes[:, j * P : (j + 1) * P].bitcast(FP8X4),
+                        lhsT_scale=scales[:, j * P : (j + 1) * P],
+                        rhs=w_codes[:].bitcast(FP8X4),
+                        rhs_scale=w_scales[:],
+                        start=(m == 0),
+                        stop=(m == MEMBERS - 1),
+                    )
+                    if m == MEMBERS - 1:
+                        res = keep.tile([P, L], F32, name="res%d" % t)
+                        nc.scalar.activation(out=res[:], in_=accs[t][:], func=ACT.Relu, scale=rinv[:, t : t + 1])
+                        nc.sync.dma_start(out=out_v[:, t, :], in_=res[:])
+
+        transposes(0)
+        quantise(0)
+        for r in range(1, len(rounds)):
+            transposes(r)
+            quantise(r)
+            if r == 3:
+                degree()
+            products(r - 1)
+        products(len(rounds) - 1)

@@ -17,20 +17,25 @@ NEIGH = 16
 MEMBERS = NEIGH + 1
 D = 512
 L = 512
+HALF = L // 2
 TILES = NODES // P
 UNITS = TILES * MEMBERS
 BANKS = UNITS // 2
-ROUND_BANKS = [2, 2] + [4] * 16
-VECTOR_EVAC = (1,)
+T_RUNS = [1, 2, 3, 4, 6, 8, 8, 9, 9, 9, 9]
+CHUNK_BANKS = [1] * 4 + [2] * 8 + [4] * 12
+VECTOR_EVERY = 4
+LAG = 2
+W_SPLIT = 336
 
 FLOPS = 2 * NODES * MEMBERS * D * L
 
-assert sum(ROUND_BANKS) == BANKS
+assert sum(T_RUNS) == BANKS
+assert sum(CHUNK_BANKS) == BANKS
 
 
 def tile_singlegcnlayer_kernel(tc, targets, neighbors, a, kernel, out):
     nc = tc.nc
-    tgt_v = targets.flatten_outer_dims().rearrange("(p t) k -> p (t k)", p=P)
+    tgt_v = targets.flatten_outer_dims().rearrange("(p t) k -> p t k", p=P)
     nb_v = neighbors.flatten_outer_dims().rearrange("(p r) k -> p (r k)", p=P)
     a_v = a.flatten_outer_dims().rearrange("(p t) m -> p (t m)", p=P)
     w_v = kernel.rearrange("(u q e) c -> q u (e c)", u=2, e=2)
@@ -38,14 +43,14 @@ def tile_singlegcnlayer_kernel(tc, targets, neighbors, a, kernel, out):
 
     rounds = []
     first = 0
-    for n in ROUND_BANKS:
+    for n in T_RUNS:
         rounds.append(list(range(first, first + n)))
         first += n
 
     with ExitStack() as ctx:
         keep = ctx.enter_context(tc.tile_pool(name="keep", bufs=1))
         gpool = ctx.enter_context(tc.tile_pool(name="gpool", bufs=8))
-        cpool = ctx.enter_context(tc.tile_pool(name="cpool", bufs=12))
+        cpool = ctx.enter_context(tc.tile_pool(name="cpool", bufs=20))
         psum_t = ctx.enter_context(tc.psum_pool(name="psum_t", bufs=6))
         psum_a = ctx.enter_context(tc.psum_pool(name="psum_a", bufs=2))
         ctx.enter_context(tc.manual_schedule())
@@ -55,28 +60,30 @@ def tile_singlegcnlayer_kernel(tc, targets, neighbors, a, kernel, out):
 
         w_raw = keep.tile([P, 4, L], BF16, name="w_raw")
         nc.sync.dma_start(out=w_raw[:].rearrange("p (u e) c -> p u (e c)", e=2), in_=w_v)
-        tgt0 = keep.tile([P, D], BF16, name="tgt0")
-        nc.sync.dma_start(out=tgt0[:], in_=tgt_v[:, 0:D])
-        tgt_rest = keep.tile([P, (TILES - 1) * D], BF16, name="tgt_rest")
         a_sb = keep.tile([P, TILES * MEMBERS], BF16, name="a_sb")
 
         words = {}
-        words[0] = tgt0[:].bitcast(F32)
-        for t in range(1, TILES):
-            words[MEMBERS * t] = tgt_rest[:].bitcast(F32)[:, (t - 1) * 256 : t * 256]
-        for r, banks in enumerate(rounds):
-            units = [g for g in range(2 * banks[0], 2 * banks[-1] + 2) if g % MEMBERS != 0]
-            flat = [(g // MEMBERS) * NEIGH + g % MEMBERS - 1 for g in units]
-            chunk = keep.tile([P, len(units) * D], BF16, name="nb%d" % r)
-            if r == 3:
-                nc.sync.dma_start(out=tgt_rest[:], in_=tgt_v[:, D:])
-                nc.sync.dma_start(out=a_sb[:], in_=a_v)
+        first = 0
+        for c, n in enumerate(CHUNK_BANKS):
+            units = list(range(2 * first, 2 * (first + n)))
+            first += n
+            nbs = [g for g in units if g % MEMBERS != NEIGH]
+            flat = [(g // MEMBERS) * NEIGH + g % MEMBERS for g in nbs]
+            chunk = keep.tile([P, len(nbs) * D], BF16, name="nb%d" % c)
             nc.sync.dma_start(out=chunk[:], in_=nb_v[:, flat[0] * D : (flat[-1] + 1) * D])
-            for i, g in enumerate(units):
+            for i, g in enumerate(nbs):
                 words[g] = chunk[:].bitcast(F32)[:, i * 256 : (i + 1) * 256]
+            for g in units:
+                if g % MEMBERS == NEIGH:
+                    tgt = keep.tile([P, D], BF16, name="tgt%d" % (g // MEMBERS))
+                    nc.sync.dma_start(out=tgt[:], in_=tgt_v[:, g // MEMBERS, :])
+                    words[g] = tgt[:].bitcast(F32)
+            if c == 4:
+                nc.sync.dma_start(out=a_sb[:], in_=a_v)
 
         w_grp = keep.tile([P, L, 4], BF16, name="w_grp", align_bytes=64)
-        nc.vector.tensor_copy(out=w_grp[:], in_=w_raw[:].rearrange("p t c -> p c t"))
+        nc.vector.tensor_copy(out=w_grp[:, :W_SPLIT, :], in_=w_raw[:, :, :W_SPLIT].rearrange("p t c -> p c t"))
+        nc.scalar.copy(out=w_grp[:, W_SPLIT:, :], in_=w_raw[:, :, W_SPLIT:].rearrange("p t c -> p c t"))
         w_codes = keep.tile([P, L], U32, name="w_codes", align_bytes=64)
         w_scales = keep.tile([P, L], U8, name="w_scales", align_bytes=64)
         nc.vector.quantize_mx(
@@ -101,8 +108,8 @@ def tile_singlegcnlayer_kernel(tc, targets, neighbors, a, kernel, out):
             nc.vector.reciprocal(out=rinv[:], in_=fac[:])
 
         banks_xt = {}
+        banks_grp = {}
         banks_q = {}
-        accs = {}
 
         def transposes(r):
             for b in rounds[r]:
@@ -112,46 +119,63 @@ def tile_singlegcnlayer_kernel(tc, targets, neighbors, a, kernel, out):
                         nc.tensor.transpose(xt[:, j, u, :], words[2 * b + j][:, u * P : (u + 1) * P], ident[:])
                 banks_xt[b] = xt
 
+        def empty(b, i):
+            grp = gpool.tile([P, 2 * D], BF16, name="grp", align_bytes=64)
+            dst = grp[:].bitcast(F32).rearrange("p (j n u) -> p j n u", j=2, u=2)
+            src = banks_xt[b][:].rearrange("p j u n -> p j n u")
+            if i % VECTOR_EVERY == 1:
+                nc.vector.tensor_copy(out=dst, in_=src)
+            else:
+                nc.scalar.copy(out=dst, in_=src)
+            banks_grp[b] = grp
+
+        def quantise_bank(b):
+            codes = cpool.tile([P, 2 * P], U32, name="codes", align_bytes=64)
+            scales = cpool.tile([P, 2 * P], U8, name="scales", align_bytes=64)
+            nc.vector.quantize_mx(out=codes[:].bitcast(FP8X4), scales=scales[:], in_=banks_grp[b][:])
+            banks_q[b] = (codes, scales)
+
         def quantise(r):
-            grouped = {}
-            for i, b in enumerate(rounds[r]):
-                grp = gpool.tile([P, 2 * D], BF16, name="grp", align_bytes=64)
-                dst = grp[:].bitcast(F32).rearrange("p (j n u) -> p j n u", j=2, u=2)
-                src = banks_xt[b][:].rearrange("p j u n -> p j n u")
-                if i in VECTOR_EVAC:
-                    nc.vector.tensor_copy(out=dst, in_=src)
-                else:
-                    nc.scalar.copy(out=dst, in_=src)
-                grouped[b] = grp
-            for b in rounds[r]:
-                codes = cpool.tile([P, 2 * P], U32, name="codes", align_bytes=64)
-                scales = cpool.tile([P, 2 * P], U8, name="scales", align_bytes=64)
-                nc.vector.quantize_mx(out=codes[:].bitcast(FP8X4), scales=scales[:], in_=grouped[b][:])
-                banks_q[b] = (codes, scales)
+            banks = rounds[r]
+            for i, b in enumerate(banks):
+                empty(b, i)
+                if i >= LAG:
+                    quantise_bank(banks[i - LAG])
+            for b in banks[max(0, len(banks) - LAG) :]:
+                quantise_bank(b)
+
+        def one_pass(acc, g, cols):
+            codes, scales = banks_q[g // 2]
+            j = g % 2
+            m = g % MEMBERS
+            nc.tensor.matmul_mx(
+                out=acc,
+                lhsT=codes[:, j * P : (j + 1) * P].bitcast(FP8X4),
+                lhsT_scale=scales[:, j * P : (j + 1) * P],
+                rhs=w_codes[:, cols].bitcast(FP8X4),
+                rhs_scale=w_scales[:, cols],
+                start=(m == 0),
+                stop=(m == MEMBERS - 1),
+            )
+
+        def finish(acc, t, cols, width, name):
+            res = keep.tile([P, width], F32, name=name)
+            nc.scalar.activation(out=res[:], in_=acc, func=ACT.Relu, scale=rinv[:, t : t + 1])
+            nc.sync.dma_start(out=out_v[:, t, cols], in_=res[:])
+
+        accs = {}
 
         def products(r):
-            for b in rounds[r]:
-                codes, scales = banks_q[b]
-                for j in range(2):
-                    g = 2 * b + j
-                    t = g // MEMBERS
-                    m = g % MEMBERS
-                    if m == 0:
-                        acc = psum_a.tile([P, L], F32, name="acc")
-                        accs[t] = acc
-                    nc.tensor.matmul_mx(
-                        out=accs[t][:],
-                        lhsT=codes[:, j * P : (j + 1) * P].bitcast(FP8X4),
-                        lhsT_scale=scales[:, j * P : (j + 1) * P],
-                        rhs=w_codes[:].bitcast(FP8X4),
-                        rhs_scale=w_scales[:],
-                        start=(m == 0),
-                        stop=(m == MEMBERS - 1),
-                    )
-                    if m == MEMBERS - 1:
-                        res = keep.tile([P, L], F32, name="res%d" % t)
-                        nc.scalar.activation(out=res[:], in_=accs[t][:], func=ACT.Relu, scale=rinv[:, t : t + 1])
-                        nc.sync.dma_start(out=out_v[:, t, :], in_=res[:])
+            for g in range(2 * rounds[r][0], 2 * rounds[r][-1] + 2):
+                t = g // MEMBERS
+                if t == TILES - 1:
+                    continue
+                if g % MEMBERS == 0:
+                    acc = psum_a.tile([P, L], F32, name="acc")
+                    accs[t] = acc
+                one_pass(accs[t][:], g, slice(0, L))
+                if g % MEMBERS == MEMBERS - 1:
+                    finish(accs[t][:], t, slice(0, L), L, "res%d" % t)
 
         transposes(0)
         quantise(0)
@@ -162,3 +186,10 @@ def tile_singlegcnlayer_kernel(tc, targets, neighbors, a, kernel, out):
                 degree()
             products(r - 1)
         products(len(rounds) - 1)
+        t = TILES - 1
+        for h in range(2):
+            cols = slice(h * HALF, (h + 1) * HALF)
+            acc = psum_a.tile([P, L], F32, name="acc")
+            for g in range(t * MEMBERS, (t + 1) * MEMBERS):
+                one_pass(acc[:, :HALF], g, cols)
+            finish(acc[:, :HALF], t, cols, HALF, "res%d_%d" % (t, h))

@@ -6,6 +6,7 @@ from concourse.masks import make_identity
 F32 = mybir.dt.float32
 BF16 = mybir.dt.bfloat16
 U32 = mybir.dt.uint32
+I32 = mybir.dt.int32
 U8 = mybir.dt.uint8
 FP8X4 = mybir.dt.float8_e4m3fn_x4
 ALU = mybir.AluOpType
@@ -19,10 +20,13 @@ D = 512
 L = 512
 HALF = L // 2
 TILES = NODES // P
-UNITS = TILES * MEMBERS
+LAST = TILES - 1
+Q = 4
+QP = P // Q
+UNITS = LAST * MEMBERS + 1
 BANKS = UNITS // 2
-T_RUNS = [1, 2, 3, 4, 6, 8, 8, 9, 9, 9, 9]
-CHUNK_BANKS = [1] * 4 + [2] * 8 + [4] * 12
+T_RUNS = [1, 2, 3, 4, 6, 8, 9, 9, 9, 9]
+CHUNK_BANKS = [1] * 4 + [2] * 8 + [4] * 10
 VECTOR_EVERY = 4
 LAG = 2
 W_SPLIT = 336
@@ -39,6 +43,7 @@ def tile_singlegcnlayer_kernel(tc, targets, neighbors, a, kernel, out):
     nb_v = neighbors.flatten_outer_dims().rearrange("(p r) k -> p (r k)", p=P)
     a_v = a.flatten_outer_dims().rearrange("(p t) m -> p (t m)", p=P)
     w_v = kernel.rearrange("(u q e) c -> q u (e c)", u=2, e=2)
+    nb_q = neighbors.flatten_outer_dims().rearrange("(b i t a m) k -> t a i b (m k)", b=Q, i=QP, t=TILES, a=Q)
     out_v = out.flatten_outer_dims().rearrange("(p t) l -> p t l", p=P)
 
     rounds = []
@@ -49,7 +54,7 @@ def tile_singlegcnlayer_kernel(tc, targets, neighbors, a, kernel, out):
 
     with ExitStack() as ctx:
         keep = ctx.enter_context(tc.tile_pool(name="keep", bufs=1))
-        gpool = ctx.enter_context(tc.tile_pool(name="gpool", bufs=8))
+        gpool = ctx.enter_context(tc.tile_pool(name="gpool", bufs=6))
         cpool = ctx.enter_context(tc.tile_pool(name="cpool", bufs=20))
         psum_t = ctx.enter_context(tc.psum_pool(name="psum_t", bufs=6))
         psum_a = ctx.enter_context(tc.psum_pool(name="psum_a", bufs=2))
@@ -58,7 +63,7 @@ def tile_singlegcnlayer_kernel(tc, targets, neighbors, a, kernel, out):
         ident = keep.tile([P, P], F32, name="ident")
         make_identity(nc, ident[:])
 
-        w_raw = keep.tile([P, 4, L], BF16, name="w_raw")
+        w_raw = keep.tile([P, 4, L], BF16, name="w_raw", align_bytes=64)
         nc.sync.dma_start(out=w_raw[:].rearrange("p (u e) c -> p u (e c)", e=2), in_=w_v)
         a_sb = keep.tile([P, TILES * MEMBERS], BF16, name="a_sb")
 
@@ -67,14 +72,14 @@ def tile_singlegcnlayer_kernel(tc, targets, neighbors, a, kernel, out):
         for c, n in enumerate(CHUNK_BANKS):
             units = list(range(2 * first, 2 * (first + n)))
             first += n
-            nbs = [g for g in units if g % MEMBERS != NEIGH]
+            nbs = [g for g in units if g % MEMBERS != NEIGH and g < LAST * MEMBERS]
             flat = [(g // MEMBERS) * NEIGH + g % MEMBERS for g in nbs]
             chunk = keep.tile([P, len(nbs) * D], BF16, name="nb%d" % c)
             nc.sync.dma_start(out=chunk[:], in_=nb_v[:, flat[0] * D : (flat[-1] + 1) * D])
             for i, g in enumerate(nbs):
                 words[g] = chunk[:].bitcast(F32)[:, i * 256 : (i + 1) * 256]
             for g in units:
-                if g % MEMBERS == NEIGH:
+                if g % MEMBERS == NEIGH or g == UNITS - 1:
                     tgt = keep.tile([P, D], BF16, name="tgt%d" % (g // MEMBERS))
                     nc.sync.dma_start(out=tgt[:], in_=tgt_v[:, g // MEMBERS, :])
                     words[g] = tgt[:].bitcast(F32)
@@ -84,11 +89,31 @@ def tile_singlegcnlayer_kernel(tc, targets, neighbors, a, kernel, out):
         w_grp = keep.tile([P, L, 4], BF16, name="w_grp", align_bytes=64)
         nc.vector.tensor_copy(out=w_grp[:, :W_SPLIT, :], in_=w_raw[:, :, :W_SPLIT].rearrange("p t c -> p c t"))
         nc.scalar.copy(out=w_grp[:, W_SPLIT:, :], in_=w_raw[:, :, W_SPLIT:].rearrange("p t c -> p c t"))
-        w_codes = keep.tile([P, L], U32, name="w_codes", align_bytes=64)
-        w_scales = keep.tile([P, L], U8, name="w_scales", align_bytes=64)
+        w_mx = keep.tile([P, 5 * L], U8, name="w_mx", align_bytes=64)
+        nc.vector.memset(w_mx[:, 4 * L :].bitcast(U32), 0)
         nc.vector.quantize_mx(
-            out=w_codes[:].bitcast(FP8X4), scales=w_scales[:], in_=w_grp[:].rearrange("p c t -> p (c t)")
+            out=w_mx[:, : 4 * L].bitcast(FP8X4), scales=w_mx[:, 4 * L :], in_=w_grp[:].rearrange("p c t -> p (c t)")
         )
+
+        def w_operand(tile):
+            return tile[:, : 4 * L].bitcast(U32), tile[:, 4 * L :]
+
+        w_all = w_operand(w_mx)
+        w_blocks = []
+        for v in range(Q):
+            spread = keep.tile([P, 5 * L], U8, name="w_mx%d" % v, align_bytes=64)
+            for qa in (0, 2, 1, 3):
+                nc.sync.dma_start(
+                    out=spread[qa * QP : (qa + 1) * QP, :].bitcast(I32),
+                    in_=w_mx[v * QP : (v + 1) * QP, :].bitcast(I32),
+                )
+            w_blocks.append(w_operand(spread))
+        quads = []
+        for b in range(Q):
+            raw = keep.tile([P, 1024], F32, name=("w_raw", "w_grp", "raw2", "raw3")[b], align_bytes=64)
+            for qa in (0, 2, 1, 3):
+                nc.sync.dma_start(out=raw[qa * QP : (qa + 1) * QP, :].bitcast(BF16), in_=nb_q[LAST, qa, :, b, :])
+            quads.append(raw)
 
         rinv = keep.tile([P, TILES], F32, name="rinv")
 
@@ -144,38 +169,58 @@ def tile_singlegcnlayer_kernel(tc, targets, neighbors, a, kernel, out):
             for b in banks[max(0, len(banks) - LAG) :]:
                 quantise_bank(b)
 
-        def one_pass(acc, g, cols):
-            codes, scales = banks_q[g // 2]
-            j = g % 2
-            m = g % MEMBERS
+        blk = keep.tile([P, Q, 1024], F32, name="blk", align_bytes=64)
+        group_in = {}
+        group_q = {}
+
+        def vector_transpose(b):
+            nc.vector.transpose(out=blk[:, b, :], in_=quads[b][:])
+
+        def group_copies(m):
+            grp = gpool.tile([P, Q * D], BF16, name="bgrp", bufs=2, align_bytes=64)
+            for v in range(Q):
+                dst = grp[:].bitcast(F32)[:, v * 256 : (v + 1) * 256].rearrange("p (b j u) -> p b j u", b=Q, u=2)
+                src = blk[:].rearrange("p b (m u v j) -> p b m u v j", m=Q, u=2, v=Q)
+                nc.scalar.copy(out=dst, in_=src[:, :, m, :, v, :].rearrange("p b u j -> p b j u"))
+            group_in[m] = grp
+
+        def quantise_group(m):
+            codes = keep.tile([P, D], U32, name="bcodes%d" % m, align_bytes=64)
+            scales = keep.tile([P, D], U8, name="bscales%d" % m, align_bytes=64)
+            nc.vector.quantize_mx(out=codes[:].bitcast(FP8X4), scales=scales[:], in_=group_in[m][:])
+            group_q[m] = (codes, scales)
+
+        def one_pass(acc, x, j, w, cols, start, stop):
+            codes, scales = x
             nc.tensor.matmul_mx(
                 out=acc,
                 lhsT=codes[:, j * P : (j + 1) * P].bitcast(FP8X4),
                 lhsT_scale=scales[:, j * P : (j + 1) * P],
-                rhs=w_codes[:, cols].bitcast(FP8X4),
-                rhs_scale=w_scales[:, cols],
-                start=(m == 0),
-                stop=(m == MEMBERS - 1),
+                rhs=w[0][:, cols].bitcast(FP8X4),
+                rhs_scale=w[1][:, cols],
+                start=start,
+                stop=stop,
             )
 
-        def finish(acc, t, cols, width, name):
-            res = keep.tile([P, width], F32, name=name)
-            nc.scalar.activation(out=res[:], in_=acc, func=ACT.Relu, scale=rinv[:, t : t + 1])
-            nc.sync.dma_start(out=out_v[:, t, cols], in_=res[:])
+        def finish(acc, t, cols, width):
+            res = gpool.tile([P, L], F32, name="res", bufs=8)
+            nc.scalar.activation(out=res[:, :width], in_=acc, func=ACT.Relu, scale=rinv[:, t : t + 1])
+            nc.sync.dma_start(out=out_v[:, t, cols], in_=res[:, :width])
 
         accs = {}
 
         def products(r):
             for g in range(2 * rounds[r][0], 2 * rounds[r][-1] + 2):
                 t = g // MEMBERS
-                if t == TILES - 1:
+                if t == LAST:
                     continue
                 if g % MEMBERS == 0:
                     acc = psum_a.tile([P, L], F32, name="acc")
                     accs[t] = acc
-                one_pass(accs[t][:], g, slice(0, L))
-                if g % MEMBERS == MEMBERS - 1:
-                    finish(accs[t][:], t, slice(0, L), L, "res%d" % t)
+                m = g % MEMBERS
+                one_pass(accs[t][:], banks_q[g // 2], g % 2, w_all, slice(0, L), m == 0, m == MEMBERS - 1)
+                if m == MEMBERS - 1:
+                    finish(accs[t][:], t, slice(0, L), L)
 
         transposes(0)
         quantise(0)
@@ -185,11 +230,21 @@ def tile_singlegcnlayer_kernel(tc, targets, neighbors, a, kernel, out):
             if r == 3:
                 degree()
             products(r - 1)
+        for b in range(Q):
+            vector_transpose(b)
+        for m in range(Q):
+            group_copies(m)
+            if m > 0:
+                quantise_group(m - 1)
+        quantise_group(Q - 1)
         products(len(rounds) - 1)
-        t = TILES - 1
+        passes = [(banks_q[BANKS - 1], 1, w_all)]
+        for m in range(Q):
+            for v in range(Q):
+                passes.append((group_q[m], v, w_blocks[v]))
         for h in range(2):
             cols = slice(h * HALF, (h + 1) * HALF)
             acc = psum_a.tile([P, L], F32, name="acc")
-            for g in range(t * MEMBERS, (t + 1) * MEMBERS):
-                one_pass(acc[:, :HALF], g, cols)
-            finish(acc[:, :HALF], t, cols, HALF, "res%d_%d" % (t, h))
+            for n, (x, j, w) in enumerate(passes):
+                one_pass(acc[:, :HALF], x, j, w, cols, n == 0, n == MEMBERS - 1)
+            finish(acc[:, :HALF], LAST, cols, HALF)

@@ -23,12 +23,20 @@ TILES = NODES // P
 LAST = TILES - 1
 Q = 4
 QP = P // Q
-UNITS = LAST * MEMBERS + 1
-BANKS = UNITS // 2
-T_RUNS = [1, 2, 3, 4, 6, 8, 9, 9, 9, 9]
-CHUNK_BANKS = [1] * 4 + [2] * 8 + [4] * 10
+MIXED = LAST - 1
+EXTRA = 0
+GROUPS = [(MIXED, g) for g in range(Q - EXTRA, Q)] + [(LAST, g) for g in range(Q)]
+UNITS = (
+    [(t, m) for t in range(MIXED) for m in range(MEMBERS)]
+    + [(MIXED, m) for m in range(NEIGH - Q * EXTRA)]
+    + [(MIXED, NEIGH), (LAST, NEIGH)]
+)
+BANKS = len(UNITS) // 2
+T_RUNS = [1, 2, 3, 4, 6, 8, 9, 9, 9, 9 - 2 * EXTRA]
+CHUNK_BANKS = [1] * 4 + [2] * 8 + [4] * 9 + [4 - 2 * EXTRA]
 VECTOR_EVERY = 4
 LAG = 2
+EARLY_GROUPS = 1
 W_SPLIT = 336
 
 FLOPS = 2 * NODES * MEMBERS * D * L
@@ -43,7 +51,7 @@ def tile_singlegcnlayer_kernel(tc, targets, neighbors, a, kernel, out):
     nb_v = neighbors.flatten_outer_dims().rearrange("(p r) k -> p (r k)", p=P)
     a_v = a.flatten_outer_dims().rearrange("(p t) m -> p (t m)", p=P)
     w_v = kernel.rearrange("(u q e) c -> q u (e c)", u=2, e=2)
-    nb_q = neighbors.flatten_outer_dims().rearrange("(b i t a m) k -> t a i b (m k)", b=Q, i=QP, t=TILES, a=Q)
+    nb_q = neighbors.flatten_outer_dims().rearrange("(b i t g a) k -> t g a i b k", b=Q, i=QP, t=TILES, a=Q)
     out_v = out.flatten_outer_dims().rearrange("(p t) l -> p t l", p=P)
 
     rounds = []
@@ -70,19 +78,20 @@ def tile_singlegcnlayer_kernel(tc, targets, neighbors, a, kernel, out):
         words = {}
         first = 0
         for c, n in enumerate(CHUNK_BANKS):
-            units = list(range(2 * first, 2 * (first + n)))
+            units = UNITS[2 * first : 2 * (first + n)]
             first += n
-            nbs = [g for g in units if g % MEMBERS != NEIGH and g < LAST * MEMBERS]
-            flat = [(g // MEMBERS) * NEIGH + g % MEMBERS for g in nbs]
-            chunk = keep.tile([P, len(nbs) * D], BF16, name="nb%d" % c)
-            nc.sync.dma_start(out=chunk[:], in_=nb_v[:, flat[0] * D : (flat[-1] + 1) * D])
-            for i, g in enumerate(nbs):
-                words[g] = chunk[:].bitcast(F32)[:, i * 256 : (i + 1) * 256]
-            for g in units:
-                if g % MEMBERS == NEIGH or g == UNITS - 1:
-                    tgt = keep.tile([P, D], BF16, name="tgt%d" % (g // MEMBERS))
-                    nc.sync.dma_start(out=tgt[:], in_=tgt_v[:, g // MEMBERS, :])
-                    words[g] = tgt[:].bitcast(F32)
+            nbs = [u for u in units if u[1] != NEIGH]
+            if nbs:
+                row = nbs[0][0] * NEIGH + nbs[0][1]
+                chunk = keep.tile([P, len(nbs) * D], BF16, name="nb%d" % c)
+                nc.sync.dma_start(out=chunk[:], in_=nb_v[:, row * D : (row + len(nbs)) * D])
+                for i, u in enumerate(nbs):
+                    words[u] = chunk[:].bitcast(F32)[:, i * 256 : (i + 1) * 256]
+            for u in units:
+                if u[1] == NEIGH:
+                    tgt = keep.tile([P, D], BF16, name="tgt%d" % u[0])
+                    nc.sync.dma_start(out=tgt[:], in_=tgt_v[:, u[0], :])
+                    words[u] = tgt[:].bitcast(F32)
             if c == 4:
                 nc.sync.dma_start(out=a_sb[:], in_=a_v)
 
@@ -108,12 +117,13 @@ def tile_singlegcnlayer_kernel(tc, targets, neighbors, a, kernel, out):
                     in_=w_mx[v * QP : (v + 1) * QP, :].bitcast(I32),
                 )
             w_blocks.append(w_operand(spread))
-        quads = []
-        for b in range(Q):
-            raw = keep.tile([P, 1024], F32, name=("w_raw", "w_grp", "raw2", "raw3")[b], align_bytes=64)
+        raws = []
+        for n, (t, g) in enumerate(GROUPS):
+            raw = keep.tile([P, 1024], F32, name="raw%d" % n if n > 1 else ("w_raw", "w_grp")[n], align_bytes=64)
+            raw_v = raw[:].bitcast(BF16).rearrange("p (b k) -> p b k", b=Q)
             for qa in (0, 2, 1, 3):
-                nc.sync.dma_start(out=raw[qa * QP : (qa + 1) * QP, :].bitcast(BF16), in_=nb_q[LAST, qa, :, b, :])
-            quads.append(raw)
+                nc.sync.dma_start(out=raw_v[qa * QP : (qa + 1) * QP, :, :], in_=nb_q[t, g, qa, :, :, :])
+            raws.append(raw)
 
         rinv = keep.tile([P, TILES], F32, name="rinv")
 
@@ -141,7 +151,7 @@ def tile_singlegcnlayer_kernel(tc, targets, neighbors, a, kernel, out):
                 xt = psum_t.tile([P, 2, 2, P], F32, name="xt")
                 for j in range(2):
                     for u in range(2):
-                        nc.tensor.transpose(xt[:, j, u, :], words[2 * b + j][:, u * P : (u + 1) * P], ident[:])
+                        nc.tensor.transpose(xt[:, j, u, :], words[UNITS[2 * b + j]][:, u * P : (u + 1) * P], ident[:])
                 banks_xt[b] = xt
 
         def empty(b, i):
@@ -169,26 +179,28 @@ def tile_singlegcnlayer_kernel(tc, targets, neighbors, a, kernel, out):
             for b in banks[max(0, len(banks) - LAG) :]:
                 quantise_bank(b)
 
-        blk = keep.tile([P, Q, 1024], F32, name="blk", align_bytes=64)
+        group_blk = {}
         group_in = {}
         group_q = {}
 
-        def vector_transpose(b):
-            nc.vector.transpose(out=blk[:, b, :], in_=quads[b][:])
+        def vector_transpose(n):
+            blk = gpool.tile([P, 1024], F32, name="blk", bufs=2, align_bytes=64)
+            nc.vector.transpose(out=blk[:], in_=raws[n][:])
+            group_blk[n] = blk
 
-        def group_copies(m):
+        def group_copies(n):
             grp = gpool.tile([P, Q * D], BF16, name="bgrp", bufs=2, align_bytes=64)
             for v in range(Q):
                 dst = grp[:].bitcast(F32)[:, v * 256 : (v + 1) * 256].rearrange("p (b j u) -> p b j u", b=Q, u=2)
-                src = blk[:].rearrange("p b (m u v j) -> p b m u v j", m=Q, u=2, v=Q)
-                nc.scalar.copy(out=dst, in_=src[:, :, m, :, v, :].rearrange("p b u j -> p b j u"))
-            group_in[m] = grp
+                src = group_blk[n][:].rearrange("p (b u v j) -> p b u v j", b=Q, u=2, v=Q)
+                nc.scalar.copy(out=dst, in_=src[:, :, :, v, :].rearrange("p b u j -> p b j u"))
+            group_in[n] = grp
 
-        def quantise_group(m):
-            codes = keep.tile([P, D], U32, name="bcodes%d" % m, align_bytes=64)
-            scales = keep.tile([P, D], U8, name="bscales%d" % m, align_bytes=64)
-            nc.vector.quantize_mx(out=codes[:].bitcast(FP8X4), scales=scales[:], in_=group_in[m][:])
-            group_q[m] = (codes, scales)
+        def quantise_group(n):
+            codes = keep.tile([P, D], U32, name="bcodes%d" % n, align_bytes=64)
+            scales = keep.tile([P, D], U8, name="bscales%d" % n, align_bytes=64)
+            nc.vector.quantize_mx(out=codes[:].bitcast(FP8X4), scales=scales[:], in_=group_in[n][:])
+            group_q[n] = (codes, scales)
 
         def one_pass(acc, x, j, w, cols, start, stop):
             codes, scales = x
@@ -208,19 +220,29 @@ def tile_singlegcnlayer_kernel(tc, targets, neighbors, a, kernel, out):
             nc.sync.dma_start(out=out_v[:, t, cols], in_=res[:, :width])
 
         accs = {}
+        done = {}
+
+        def member_pass(t, x, j, w):
+            n = done.setdefault(t, 0)
+            if n == 0:
+                acc = psum_a.tile([P, L], F32, name="acc")
+                accs[t] = acc
+            one_pass(accs[t][:], x, j, w, slice(0, L), n == 0, n == MEMBERS - 1)
+            done[t] = n + 1
+            if n == MEMBERS - 1:
+                finish(accs[t][:], t, slice(0, L), L)
 
         def products(r):
             for g in range(2 * rounds[r][0], 2 * rounds[r][-1] + 2):
-                t = g // MEMBERS
-                if t == LAST:
-                    continue
-                if g % MEMBERS == 0:
-                    acc = psum_a.tile([P, L], F32, name="acc")
-                    accs[t] = acc
-                m = g % MEMBERS
-                one_pass(accs[t][:], banks_q[g // 2], g % 2, w_all, slice(0, L), m == 0, m == MEMBERS - 1)
-                if m == MEMBERS - 1:
-                    finish(accs[t][:], t, slice(0, L), L)
+                if UNITS[g][0] != LAST:
+                    member_pass(UNITS[g][0], banks_q[g // 2], g % 2, w_all)
+
+        def groups(numbers):
+            for n in numbers:
+                vector_transpose(n)
+                if n > 0:
+                    quantise_group(n - 1)
+                group_copies(n)
 
         transposes(0)
         quantise(0)
@@ -229,19 +251,19 @@ def tile_singlegcnlayer_kernel(tc, targets, neighbors, a, kernel, out):
             quantise(r)
             if r == 3:
                 degree()
+            if r == len(rounds) - 1:
+                groups(range(EARLY_GROUPS))
             products(r - 1)
-        for b in range(Q):
-            vector_transpose(b)
-        for m in range(Q):
-            group_copies(m)
-            if m > 0:
-                quantise_group(m - 1)
-        quantise_group(Q - 1)
+        groups(range(EARLY_GROUPS, len(GROUPS)))
+        quantise_group(len(GROUPS) - 1)
         products(len(rounds) - 1)
-        passes = [(banks_q[BANKS - 1], 1, w_all)]
-        for m in range(Q):
+        for n in range(EXTRA):
             for v in range(Q):
-                passes.append((group_q[m], v, w_blocks[v]))
+                member_pass(MIXED, group_q[n], v, w_blocks[v])
+        passes = [(banks_q[BANKS - 1], 1, w_all)]
+        for n in range(EXTRA, len(GROUPS)):
+            for v in range(Q):
+                passes.append((group_q[n], v, w_blocks[v]))
         for h in range(2):
             cols = slice(h * HALF, (h + 1) * HALF)
             acc = psum_a.tile([P, L], F32, name="acc")

@@ -36,7 +36,8 @@ T_RUNS = [1, 2, 3, 4, 6, 8, 9, 9, 9, 9 - 2 * EXTRA]
 CHUNK_BANKS = [1] * 4 + [2] * 8 + [4] * 9 + [4 - 2 * EXTRA]
 VECTOR_EVERY = 4
 LAG = 2
-EARLY_GROUPS = 1
+COPIES_BEHIND = UNITS.index((LAST - 3, NEIGH))
+EARLY_AT = [4, 7]
 W_SPLIT = 336
 
 FLOPS = 2 * NODES * MEMBERS * D * L
@@ -176,6 +177,8 @@ def tile_singlegcnlayer_kernel(tc, targets, neighbors, a, kernel, out):
                 empty(b, i)
                 if i >= LAG:
                     quantise_bank(banks[i - LAG])
+                if r == len(rounds) - 1 and i in EARLY_AT:
+                    vector_transpose(EARLY_AT.index(i))
             for b in banks[max(0, len(banks) - LAG) :]:
                 quantise_bank(b)
 
@@ -236,13 +239,9 @@ def tile_singlegcnlayer_kernel(tc, targets, neighbors, a, kernel, out):
             for g in range(2 * rounds[r][0], 2 * rounds[r][-1] + 2):
                 if UNITS[g][0] != LAST:
                     member_pass(UNITS[g][0], banks_q[g // 2], g % 2, w_all)
-
-        def groups(numbers):
-            for n in numbers:
-                vector_transpose(n)
-                if n > 0:
-                    quantise_group(n - 1)
-                group_copies(n)
+                if g == COPIES_BEHIND:
+                    group_copies(0)
+                    group_copies(1)
 
         transposes(0)
         quantise(0)
@@ -251,10 +250,12 @@ def tile_singlegcnlayer_kernel(tc, targets, neighbors, a, kernel, out):
             quantise(r)
             if r == 3:
                 degree()
-            if r == len(rounds) - 1:
-                groups(range(EARLY_GROUPS))
             products(r - 1)
-        groups(range(EARLY_GROUPS, len(GROUPS)))
+        for n in range(2, len(GROUPS)):
+            vector_transpose(n)
+            quantise_group(n - 2)
+            group_copies(n)
+        quantise_group(len(GROUPS) - 2)
         quantise_group(len(GROUPS) - 1)
         products(len(rounds) - 1)
         for n in range(EXTRA):

@@ -99,7 +99,7 @@ def tile_singlegcnlayer_kernel(tc, targets, neighbors, a, kernel, out):
         w_grp = keep.tile([P, L, 4], BF16, name="w_grp", align_bytes=64)
         nc.vector.tensor_copy(out=w_grp[:, :W_SPLIT, :], in_=w_raw[:, :, :W_SPLIT].rearrange("p t c -> p c t"))
         nc.scalar.copy(out=w_grp[:, W_SPLIT:, :], in_=w_raw[:, :, W_SPLIT:].rearrange("p t c -> p c t"))
-        w_mx = keep.tile([P, 5 * L], U8, name="w_mx", align_bytes=64)
+        w_mx = keep.tile([P, 5 * L], U8, name="w_mx", align_bytes=256)
         nc.vector.memset(w_mx[:, 4 * L :].bitcast(U32), 0)
         nc.vector.quantize_mx(
             out=w_mx[:, : 4 * L].bitcast(FP8X4), scales=w_mx[:, 4 * L :], in_=w_grp[:].rearrange("p c t -> p (c t)")
@@ -111,7 +111,7 @@ def tile_singlegcnlayer_kernel(tc, targets, neighbors, a, kernel, out):
         w_all = w_operand(w_mx)
         w_blocks = []
         for v in range(Q):
-            spread = keep.tile([P, 5 * L], U8, name="w_mx%d" % v, align_bytes=64)
+            spread = keep.tile([P, 5 * L], U8, name="w_mx%d" % v, align_bytes=256)
             for qa in (0, 2, 1, 3):
                 nc.sync.dma_start(
                     out=spread[qa * QP : (qa + 1) * QP, :].bitcast(I32),
@@ -166,8 +166,8 @@ def tile_singlegcnlayer_kernel(tc, targets, neighbors, a, kernel, out):
             banks_grp[b] = grp
 
         def quantise_bank(b):
-            codes = cpool.tile([P, 2 * P], U32, name="codes", align_bytes=64)
-            scales = cpool.tile([P, 2 * P], U8, name="scales", align_bytes=64)
+            codes = cpool.tile([P, 2 * P], U32, name="codes", align_bytes=256)
+            scales = cpool.tile([P, 2 * P], U8, name="scales", align_bytes=256)
             nc.vector.quantize_mx(out=codes[:].bitcast(FP8X4), scales=scales[:], in_=banks_grp[b][:])
             banks_q[b] = (codes, scales)
 
@@ -200,8 +200,8 @@ def tile_singlegcnlayer_kernel(tc, targets, neighbors, a, kernel, out):
             group_in[n] = grp
 
         def quantise_group(n):
-            codes = keep.tile([P, D], U32, name="bcodes%d" % n, align_bytes=64)
-            scales = keep.tile([P, D], U8, name="bscales%d" % n, align_bytes=64)
+            codes = keep.tile([P, D], U32, name="bcodes%d" % n, align_bytes=256)
+            scales = keep.tile([P, D], U8, name="bscales%d" % n, align_bytes=256)
             nc.vector.quantize_mx(out=codes[:].bitcast(FP8X4), scales=scales[:], in_=group_in[n][:])
             group_q[n] = (codes, scales)
 

@@ -36,6 +36,7 @@ T_RUNS = [1, 2, 3, 4, 6, 8, 9, 9, 9, 9 - 2 * EXTRA]
 CHUNK_BANKS = [1] * 4 + [2] * 8 + [4] * 9 + [4 - 2 * EXTRA]
 VECTOR_EVERY = 4
 LAG = 2
+SPREAD_ROUNDS = [3, 4, 5, 6]
 COPIES_BEHIND = UNITS.index((LAST - 3, NEIGH))
 EARLY_AT = [4, 7]
 W_SPLIT = 336
@@ -99,32 +100,39 @@ def tile_singlegcnlayer_kernel(tc, targets, neighbors, a, kernel, out):
         w_grp = keep.tile([P, L, 4], BF16, name="w_grp", align_bytes=64)
         nc.vector.tensor_copy(out=w_grp[:, :W_SPLIT, :], in_=w_raw[:, :, :W_SPLIT].rearrange("p t c -> p c t"))
         nc.scalar.copy(out=w_grp[:, W_SPLIT:, :], in_=w_raw[:, :, W_SPLIT:].rearrange("p t c -> p c t"))
-        w_mx = keep.tile([P, 5 * L], U8, name="w_mx", align_bytes=256)
-        nc.vector.memset(w_mx[:, 4 * L :].bitcast(U32), 0)
-        nc.vector.quantize_mx(
-            out=w_mx[:, : 4 * L].bitcast(FP8X4), scales=w_mx[:, 4 * L :], in_=w_grp[:].rearrange("p c t -> p (c t)")
-        )
+        def quantise_w(name):
+            both = keep.tile([P, 5 * L], U8, name=name, align_bytes=256)
+            nc.vector.memset(both[:, 4 * L :].bitcast(U32), 0)
+            nc.vector.quantize_mx(
+                out=both[:, : 4 * L].bitcast(FP8X4), scales=both[:, 4 * L :], in_=w_grp[:].rearrange("p c t -> p (c t)")
+            )
+            return both
 
-        def w_operand(tile):
-            return tile[:, : 4 * L].bitcast(U32), tile[:, 4 * L :]
+        def w_operand(both):
+            return both[:, : 4 * L].bitcast(U32), both[:, 4 * L :]
 
+        w_mx = quantise_w("w_mx")
         w_all = w_operand(w_mx)
         w_blocks = []
-        for v in range(Q):
-            spread = keep.tile([P, 5 * L], U8, name="w_mx%d" % v, align_bytes=256)
-            for qa in (0, 2, 1, 3):
-                nc.sync.dma_start(
-                    out=spread[qa * QP : (qa + 1) * QP, :].bitcast(I32),
-                    in_=w_mx[v * QP : (v + 1) * QP, :].bitcast(I32),
-                )
-            w_blocks.append(w_operand(spread))
         raws = []
-        for n, (t, g) in enumerate(GROUPS):
-            raw = keep.tile([P, 1024], F32, name="raw%d" % n if n > 1 else ("w_raw", "w_grp")[n], align_bytes=64)
-            raw_v = raw[:].bitcast(BF16).rearrange("p (b k) -> p b k", b=Q)
-            for qa in (0, 2, 1, 3):
-                nc.sync.dma_start(out=raw_v[qa * QP : (qa + 1) * QP, :, :], in_=nb_q[t, g, qa, :, :, :])
-            raws.append(raw)
+
+        def spread_w(v):
+            both = quantise_w("w_mx%d" % v)
+            for qa in range(Q):
+                if qa != v:
+                    nc.sync.dma_start(
+                        out=both[qa * QP : (qa + 1) * QP, :].bitcast(I32),
+                        in_=w_mx[v * QP : (v + 1) * QP, :].bitcast(I32),
+                    )
+            w_blocks.append(w_operand(both))
+
+        def load_groups():
+            for n, (t, g) in enumerate(GROUPS):
+                raw = keep.tile([P, 1024], F32, name="raw%d" % n if n > 1 else ("w_raw", "w_grp")[n], align_bytes=64)
+                raw_v = raw[:].bitcast(BF16).rearrange("p (b k) -> p b k", b=Q)
+                for qa in (0, 2, 1, 3):
+                    nc.sync.dma_start(out=raw_v[qa * QP : (qa + 1) * QP, :, :], in_=nb_q[t, g, qa, :, :, :])
+                raws.append(raw)
 
         rinv = keep.tile([P, TILES], F32, name="rinv")
 
@@ -250,6 +258,10 @@ def tile_singlegcnlayer_kernel(tc, targets, neighbors, a, kernel, out):
             quantise(r)
             if r == 3:
                 degree()
+            if r in SPREAD_ROUNDS:
+                spread_w(SPREAD_ROUNDS.index(r))
+            if r == SPREAD_ROUNDS[-1]:
+                load_groups()
             products(r - 1)
         for n in range(2, len(GROUPS)):
             vector_transpose(n)

from contextlib import ExitStack

import concourse.mybir as mybir
from concourse.masks import make_identity

F32 = mybir.dt.float32
BF16 = mybir.dt.bfloat16
U32 = mybir.dt.uint32
I32 = mybir.dt.int32
U8 = mybir.dt.uint8
FP8X4 = mybir.dt.float8_e4m3fn_x4
ALU = mybir.AluOpType
ACT = mybir.ActivationFunctionType

P = 128
NODES = 1024
NEIGH = 16
MEMBERS = NEIGH + 1
D = 512
L = 512
HALF = L // 2
TILES = NODES // P
LAST = TILES - 1
Q = 4
QP = P // Q
MIXED = LAST - 1
EXTRA = 0
GROUPS = [(MIXED, g) for g in range(Q - EXTRA, Q)] + [(LAST, g) for g in range(Q)]
UNITS = (
    [(t, m) for t in range(MIXED) for m in range(MEMBERS)]
    + [(MIXED, m) for m in range(NEIGH - Q * EXTRA)]
    + [(MIXED, NEIGH), (LAST, NEIGH)]
)
BANKS = len(UNITS) // 2
T_RUNS = [1, 2, 3, 4, 6, 8, 9, 9, 9, 9 - 2 * EXTRA]
CHUNK_BANKS = [1] * 4 + [2] * 8 + [4] * 9 + [4 - 2 * EXTRA]
VECTOR_EVERY = 4
LAG = 2
SPREAD_ROUNDS = [3, 4, 5, 6]
COPIES_BEHIND = UNITS.index((LAST - 3, NEIGH))
EARLY_AT = [4, 7]
W_SPLIT = 336

FLOPS = 2 * NODES * MEMBERS * D * L

assert sum(T_RUNS) == BANKS
assert sum(CHUNK_BANKS) == BANKS


def tile_singlegcnlayer_kernel(tc, targets, neighbors, a, kernel, out):
    nc = tc.nc
    tgt_v = targets.flatten_outer_dims().rearrange("(p t) k -> p t k", p=P)
    nb_v = neighbors.flatten_outer_dims().rearrange("(p r) k -> p (r k)", p=P)
    a_v = a.flatten_outer_dims().rearrange("(p t) m -> p (t m)", p=P)
    w_v = kernel.rearrange("(u q e) c -> q u (e c)", u=2, e=2)
    nb_q = neighbors.flatten_outer_dims().rearrange("(b i t g a) k -> t g a i b k", b=Q, i=QP, t=TILES, a=Q)
    out_v = out.flatten_outer_dims().rearrange("(p t) l -> p t l", p=P)

    rounds = []
    first = 0
    for n in T_RUNS:
        rounds.append(list(range(first, first + n)))
        first += n

    with ExitStack() as ctx:
        keep = ctx.enter_context(tc.tile_pool(name="keep", bufs=1))
        gpool = ctx.enter_context(tc.tile_pool(name="gpool", bufs=6))
        cpool = ctx.enter_context(tc.tile_pool(name="cpool", bufs=20))
        psum_t = ctx.enter_context(tc.psum_pool(name="psum_t", bufs=6))
        psum_a = ctx.enter_context(tc.psum_pool(name="psum_a", bufs=2))
        ctx.enter_context(tc.manual_schedule())

        ident = keep.tile([P, P], F32, name="ident")
        make_identity(nc, ident[:])

        w_raw = keep.tile([P, 4, L], BF16, name="w_raw", align_bytes=64)
        nc.sync.dma_start(out=w_raw[:].rearrange("p (u e) c -> p u (e c)", e=2), in_=w_v)
        a_sb = keep.tile([P, TILES * MEMBERS], BF16, name="a_sb")

        words = {}
        first = 0
        for c, n in enumerate(CHUNK_BANKS):
            units = UNITS[2 * first : 2 * (first + n)]
            first += n
            nbs = [u for u in units if u[1] != NEIGH]
            if nbs:
                row = nbs[0][0] * NEIGH + nbs[0][1]
                chunk = keep.tile([P, len(nbs) * D], BF16, name="nb%d" % c)
                nc.sync.dma_start(out=chunk[:], in_=nb_v[:, row * D : (row + len(nbs)) * D])
                for i, u in enumerate(nbs):
                    words[u] = chunk[:].bitcast(F32)[:, i * 256 : (i + 1) * 256]
            for u in units:
                if u[1] == NEIGH:
                    tgt = keep.tile([P, D], BF16, name="tgt%d" % u[0])
                    nc.sync.dma_start(out=tgt[:], in_=tgt_v[:, u[0], :])
                    words[u] = tgt[:].bitcast(F32)
            if c == 4:
                nc.sync.dma_start(out=a_sb[:], in_=a_v)

        w_grp = keep.tile([P, L, 4], BF16, name="w_grp", align_bytes=64)
        nc.vector.tensor_copy(out=w_grp[:, :W_SPLIT, :], in_=w_raw[:, :, :W_SPLIT].rearrange("p t c -> p c t"))
        nc.scalar.copy(out=w_grp[:, W_SPLIT:, :], in_=w_raw[:, :, W_SPLIT:].rearrange("p t c -> p c t"))
        def quantise_w(name):
            both = keep.tile([P, 5 * L], U8, name=name, align_bytes=256)
            nc.vector.memset(both[:, 4 * L :].bitcast(U32), 0)
            nc.vector.quantize_mx(
                out=both[:, : 4 * L].bitcast(FP8X4), scales=both[:, 4 * L :], in_=w_grp[:].rearrange("p c t -> p (c t)")
            )
            return both

        def w_operand(both):
            return both[:, : 4 * L].bitcast(U32), both[:, 4 * L :]

        w_mx = quantise_w("w_mx")
        w_all = w_operand(w_mx)
        w_blocks = []
        raws = []

        def spread_w(v):
            both = quantise_w("w_mx%d" % v)
            for qa in range(Q):
                if qa != v:
                    nc.sync.dma_start(
                        out=both[qa * QP : (qa + 1) * QP, :].bitcast(I32),
                        in_=w_mx[v * QP : (v + 1) * QP, :].bitcast(I32),
                    )
            w_blocks.append(w_operand(both))

        def load_groups():
            for n, (t, g) in enumerate(GROUPS):
                raw = keep.tile([P, 1024], F32, name="raw%d" % n if n > 1 else ("w_raw", "w_grp")[n], align_bytes=64)
                raw_v = raw[:].bitcast(BF16).rearrange("p (b k) -> p b k", b=Q)
                for qa in (0, 2, 1, 3):
                    nc.sync.dma_start(out=raw_v[qa * QP : (qa + 1) * QP, :, :], in_=nb_q[t, g, qa, :, :, :])
                raws.append(raw)

        rinv = keep.tile([P, TILES], F32, name="rinv")

        def degree():
            deg = keep.tile([P, TILES], F32, name="deg")
            nc.vector.tensor_reduce(
                out=deg[:], in_=a_sb[:].rearrange("p (t m) -> p t m", m=MEMBERS), axis=mybir.AxisListType.X, op=ALU.add
            )
            big = keep.tile([P, TILES], F32, name="big")
            nc.vector.tensor_scalar(out=big[:], in0=deg[:], scalar1=0.5, scalar2=None, op0=ALU.is_gt)
            kept = keep.tile([P, TILES], F32, name="kept")
            nc.vector.tensor_tensor(out=kept[:], in0=deg[:], in1=big[:], op=ALU.mult)
            small = keep.tile([P, TILES], F32, name="small")
            nc.vector.tensor_scalar(out=small[:], in0=big[:], scalar1=-1.0, scalar2=1.0, op0=ALU.mult, op1=ALU.add)
            fac = keep.tile([P, TILES], F32, name="fac")
            nc.vector.tensor_tensor(out=fac[:], in0=kept[:], in1=small[:], op=ALU.max)
            nc.vector.reciprocal(out=rinv[:], in_=fac[:])

        banks_xt = {}
        banks_grp = {}
        banks_q = {}

        def transposes(r):
            for b in rounds[r]:
                xt = psum_t.tile([P, 2, 2, P], F32, name="xt")
                for j in range(2):
                    for u in range(2):
                        nc.tensor.transpose(xt[:, j, u, :], words[UNITS[2 * b + j]][:, u * P : (u + 1) * P], ident[:])
                banks_xt[b] = xt

        def empty(b, i):
            grp = gpool.tile([P, 2 * D], BF16, name="grp", align_bytes=64)
            dst = grp[:].bitcast(F32).rearrange("p (j n u) -> p j n u", j=2, u=2)
            src = banks_xt[b][:].rearrange("p j u n -> p j n u")
            if i % VECTOR_EVERY == 1:
                nc.vector.tensor_copy(out=dst, in_=src)
            else:
                nc.scalar.copy(out=dst, in_=src)
            banks_grp[b] = grp

        def quantise_bank(b):
            codes = cpool.tile([P, 2 * P], U32, name="codes", align_bytes=256)
            scales = cpool.tile([P, 2 * P], U8, name="scales", align_bytes=256)
            nc.vector.quantize_mx(out=codes[:].bitcast(FP8X4), scales=scales[:], in_=banks_grp[b][:])
            banks_q[b] = (codes, scales)

        def quantise(r):
            banks = rounds[r]
            for i, b in enumerate(banks):
                empty(b, i)
                if i >= LAG:
                    quantise_bank(banks[i - LAG])
                if r == len(rounds) - 1 and i in EARLY_AT:
                    vector_transpose(EARLY_AT.index(i))
            for b in banks[max(0, len(banks) - LAG) :]:
                quantise_bank(b)

        group_blk = {}
        group_in = {}
        group_q = {}

        def vector_transpose(n):
            blk = gpool.tile([P, 1024], F32, name="blk", bufs=2, align_bytes=64)
            nc.vector.transpose(out=blk[:], in_=raws[n][:])
            group_blk[n] = blk

        def group_copies(n):
            grp = gpool.tile([P, Q * D], BF16, name="bgrp", bufs=2, align_bytes=64)
            for v in range(Q):
                dst = grp[:].bitcast(F32)[:, v * 256 : (v + 1) * 256].rearrange("p (b j u) -> p b j u", b=Q, u=2)
                src = group_blk[n][:].rearrange("p (b u v j) -> p b u v j", b=Q, u=2, v=Q)
                nc.scalar.copy(out=dst, in_=src[:, :, :, v, :].rearrange("p b u j -> p b j u"))
            group_in[n] = grp

        def quantise_group(n):
            codes = keep.tile([P, D], U32, name="bcodes%d" % n, align_bytes=256)
            scales = keep.tile([P, D], U8, name="bscales%d" % n, align_bytes=256)
            nc.vector.quantize_mx(out=codes[:].bitcast(FP8X4), scales=scales[:], in_=group_in[n][:])
            group_q[n] = (codes, scales)

        def one_pass(acc, x, j, w, cols, start, stop):
            codes, scales = x
            nc.tensor.matmul_mx(
                out=acc,
                lhsT=codes[:, j * P : (j + 1) * P].bitcast(FP8X4),
                lhsT_scale=scales[:, j * P : (j + 1) * P],
                rhs=w[0][:, cols].bitcast(FP8X4),
                rhs_scale=w[1][:, cols],
                start=start,
                stop=stop,
            )

        def finish(acc, t, cols, width):
            res = gpool.tile([P, L], F32, name="res", bufs=8)
            nc.scalar.activation(out=res[:, :width], in_=acc, func=ACT.Relu, scale=rinv[:, t : t + 1])
            nc.sync.dma_start(out=out_v[:, t, cols], in_=res[:, :width])

        accs = {}
        done = {}

        def member_pass(t, x, j, w):
            n = done.setdefault(t, 0)
            if n == 0:
                acc = psum_a.tile([P, L], F32, name="acc")
                accs[t] = acc
            one_pass(accs[t][:], x, j, w, slice(0, L), n == 0, n == MEMBERS - 1)
            done[t] = n + 1
            if n == MEMBERS - 1:
                finish(accs[t][:], t, slice(0, L), L)

        def products(r):
            for g in range(2 * rounds[r][0], 2 * rounds[r][-1] + 2):
                if UNITS[g][0] != LAST:
                    member_pass(UNITS[g][0], banks_q[g // 2], g % 2, w_all)
                if g == COPIES_BEHIND:
                    group_copies(0)
                    group_copies(1)

        transposes(0)
        quantise(0)
        for r in range(1, len(rounds)):
            transposes(r)
            quantise(r)
            if r == 3:
                degree()
            if r in SPREAD_ROUNDS:
                spread_w(SPREAD_ROUNDS.index(r))
            if r == SPREAD_ROUNDS[-1]:
                load_groups()
            products(r - 1)
        for n in range(2, len(GROUPS)):
            vector_transpose(n)
            quantise_group(n - 2)
            group_copies(n)
        quantise_group(len(GROUPS) - 2)
        quantise_group(len(GROUPS) - 1)
        products(len(rounds) - 1)
        for n in range(EXTRA):
            for v in range(Q):
                member_pass(MIXED, group_q[n], v, w_blocks[v])
        passes = [(banks_q[BANKS - 1], 1, w_all)]
        for n in range(EXTRA, len(GROUPS)):
            for v in range(Q):
                passes.append((group_q[n], v, w_blocks[v]))
        for h in range(2):
            cols = slice(h * HALF, (h + 1) * HALF)
            acc = psum_a.tile([P, L], F32, name="acc")
            for n, (x, j, w) in enumerate(passes):
                one_pass(acc[:, :HALF], x, j, w, cols, n == 0, n == MEMBERS - 1)
            finish(acc[:, :HALF], LAST, cols, HALF)
